import numpy as np
import ml_dtypes


def mxq(x, axis, fmt="e4m3"):
    dtype, down = {"e4m3": (ml_dtypes.float8_e4m3fn, 7), "e5m2": (ml_dtypes.float8_e5m2, 14)}[fmt]
    v = np.moveaxis(np.asarray(x, np.float32).astype(ml_dtypes.bfloat16).astype(np.float64), axis, -1)
    blocks = v.reshape(v.shape[:-1] + (-1, 32))
    amax = np.abs(blocks).max(-1, keepdims=True)
    byte = np.maximum(np.where(amax > 0, np.frexp(amax)[1] - 1 + 127, 0) - down, 1)
    scale = np.exp2(byte - 127.0)
    codes = (blocks / scale).astype(np.float32).astype(dtype).astype(np.float64)
    return np.moveaxis((codes * scale).reshape(v.shape), -1, axis)


WIDE = False


def mx_kscale(k):
    if not WIDE:
        return np.ones(k)
    levels = np.array([10, -10, 5, -5, 0])
    a = np.random.permutation(np.resize(levels, k // 512 * 4)).reshape(k // 512, 4)
    idx = np.arange(k)
    return np.exp2(a[idx // 512, idx % 128 // 32])


BF16 = ml_dtypes.bfloat16


def bf(x):
    return np.asarray(x, np.float32).astype(BF16)


def f64(x):
    return np.asarray(x).astype(np.float64)


B, S, D, E = 2, 512, 512, 512
EPS = 1e-5


def layer_norm(x, g, b):
    mu = x.mean(-1, keepdims=True)
    var = np.square(x - mu).mean(-1, keepdims=True)
    return (x - mu) / np.sqrt(var + EPS) * g + b


def setup_inputs():
    s = mx_kscale(D)

    def stream():
        return bf(np.random.standard_normal((B, S, D)) + 0.5 * np.random.standard_normal((B, S, 1)))

    def gain():
        return bf((1.0 + 0.1 * np.random.standard_normal(D)) * s)

    def shift():
        return bf(0.1 * np.random.standard_normal(D) * s)

    def weight(a):
        return bf(np.random.standard_normal((E, D)) * a / np.sqrt(D) / s[None, :])

    def bias():
        return bf(0.2 * np.random.standard_normal(E))

    return {"text": stream(), "img": stream(),
            "ln_t_g": gain(), "ln_t_b": shift(), "ln_i_g": gain(), "ln_i_b": shift(),
            "Wq": weight(1.5), "bq": bias(),
            "Wkt": weight(1.5), "bkt": bias(), "Wvt": weight(1.0), "bvt": bias(),
            "Wki": weight(1.5), "bki": bias(), "Wvi": weight(1.0), "bvi": bias()}


def reference(text, img, ln_t_g, ln_t_b, ln_i_g, ln_i_b, Wq, bq, Wkt, bkt, Wvt, bvt, Wki, bki, Wvi, bvi):
    tn = mxq(layer_norm(f64(text), f64(ln_t_g), f64(ln_t_b)), 2, "e4m3")
    im = mxq(layer_norm(f64(img), f64(ln_i_g), f64(ln_i_b)), 2, "e4m3")
    wq = mxq(f64(Wq), 1, "e4m3").T
    q = np.concatenate([(tn @ wq), (im @ wq)], 0) + f64(bq)
    k = np.concatenate([(tn @ mxq(f64(Wkt), 1, "e4m3").T) + f64(bkt), (im @ mxq(f64(Wki), 1, "e4m3").T) + f64(bki)], 0)
    v = np.concatenate([(tn @ mxq(f64(Wvt), 1, "e4m3").T) + f64(bvt), (im @ mxq(f64(Wvi), 1, "e4m3").T) + f64(bvi)], 0)
    return q, k, v

@@ -1,0 +1,251 @@
+from contextlib import ExitStack
+
+import concourse.mybir as mybir
+from concourse.masks import make_identity
+
+F32 = mybir.dt.float32
+BF16 = mybir.dt.bfloat16
+U32 = mybir.dt.uint32
+U8 = mybir.dt.uint8
+FP8X4 = mybir.dt.float8_e4m3fn_x4
+ACT = mybir.ActivationFunctionType
+ALU = mybir.AluOpType
+
+P = 128
+PACK = 4
+D = P * PACK
+E = 512
+TILES = 8
+GROUP = 2
+GROUPS = 2 * TILES // GROUP
+TOKENS = GROUP * P
+STATS_AHEAD = 6
+EPS = 1e-5
+
+FLOPS = 2 * 2 * TILES * P * D * 3 * E
+
+
+def tile_modalityadaptivemodule_pa_kernel(
+    tc, text, img, ln_t_g, ln_t_b, ln_i_g, ln_i_b,
+    Wq, bq, Wkt, bkt, Wvt, bvt, Wki, bki, Wvi, bvi,
+    out_0, out_1, out_2,
+):
+    nc = tc.nc
+    streams = [text, img]
+    ln_vectors = [ln_t_g, ln_t_b, ln_i_g, ln_i_b]
+    weights = [Wq, Wkt, Wvt, Wki, Wvi]
+    biases = [bq, bkt, bvt, bki, bvi]
+    qkv_of_stream = [(0, 1, 2), (0, 3, 4)]
+    x_dram = [x.flatten_outer_dims().rearrange("(p t) d -> p t d", p=P) for x in streams]
+    out_dram = [o.flatten_outer_dims().rearrange("(s p t) e -> s p t e", s=2, p=P) for o in (out_0, out_1, out_2)]
+
+    def stream_of(n):
+        return n // (GROUPS // 2)
+
+    def tiles_of(n):
+        first = (n % (GROUPS // 2)) * GROUP
+        return slice(first, first + GROUP)
+
+    with ExitStack() as ctx:
+        ctx.enter_context(tc.manual_schedule())
+        keep = ctx.enter_context(tc.tile_pool(name="keep", bufs=1))
+        small = ctx.enter_context(tc.tile_pool(name="small", bufs=STATS_AHEAD))
+        work = ctx.enter_context(tc.tile_pool(name="work", bufs=2))
+        results = ctx.enter_context(tc.tile_pool(name="results", bufs=4))
+        flip = ctx.enter_context(tc.psum_pool(name="flip", bufs=2))
+        sums = ctx.enter_context(tc.psum_pool(name="sums", bufs=6))
+
+        ident = keep.tile([P, P], F32)
+        make_identity(nc, ident[:])
+        ln_rows = keep.tile([P, D // 2], BF16)
+        nc.vector.memset(ln_rows[:], 0.0)
+        bias_rows = keep.tile([P, 5, E], BF16)
+        nc.vector.memset(bias_rows[:], 0.0)
+        ones = keep.tile([P, P], BF16)
+        nc.vector.memset(ones[:], 1.0)
+        eps = keep.tile([P, 1], F32)
+        nc.vector.memset(eps[:], EPS)
+
+        x_sb = [keep.tile([P, TILES, D], BF16, name="x_sb%d" % s) for s in range(2)]
+        w_sb = [keep.tile([P, E // P, D], BF16, name="w_sb%d" % j) for j in range(5)]
+
+        def load_tokens(n):
+            s = stream_of(n)
+            nc.sync.dma_start(out=x_sb[s][:, tiles_of(n), :], in_=x_dram[s][:, tiles_of(n), :])
+
+        def load_weight(j):
+            nc.sync.dma_start(out=w_sb[j][:], in_=weights[j].rearrange("(c p) d -> p c d", p=P))
+
+        for v in range(4):
+            nc.scalar.dma_start(out=ln_rows[2 * v : 2 * v + 2, :], in_=ln_vectors[v].rearrange("(u w) -> u w", u=2))
+        load_tokens(0)
+        load_tokens(1)
+        for j in range(5):
+            load_weight(j)
+            nc.sync.dma_start(out=bias_rows[0:1, j, :], in_=biases[j].rearrange("(o e) -> o e", o=1))
+            load_tokens(j + 2)
+        load_tokens(7)
+
+        ln_cols = keep.tile([P, 4 * PACK], F32)
+
+        def spread_layer_norm_vectors():
+            ln_bank = flip.tile([P, P], F32, tag="flip")
+            nc.tensor.transpose(ln_bank[:], ln_rows[:].bitcast(F32), ident[:])
+            nc.scalar.copy(out=ln_cols[:], in_=ln_bank[:, 0:8].bitcast(BF16))
+
+        w_codes = keep.tile([P, 5, E], U32, align_bytes=64)
+        w_scales = keep.tile([P, 5, E], U8, align_bytes=64)
+        bias_all = keep.tile([P, 5, E], BF16)
+
+        def prepare_weight(j):
+            w_grouped = work.tile([P, E * PACK], BF16, align_bytes=64)
+            w_words = w_grouped[:].bitcast(F32).rearrange("p (r u) -> p r u", u=2)
+            for half in range(2):
+                bank = flip.tile([P, 2, 2 * P], F32, tag="flip")
+                for c in range(2):
+                    rows_as_words = w_sb[j][:, 2 * half + c, :].bitcast(F32)
+                    for u in range(2):
+                        nc.tensor.transpose(bank[:, u, c * P : (c + 1) * P], rows_as_words[:, u * P : (u + 1) * P], ident[:])
+                nc.scalar.copy(out=w_words[:, half * 2 * P : (half + 1) * 2 * P, :], in_=bank[:].rearrange("p u r -> p r u"))
+            nc.vector.quantize_mx(out=w_codes[:, j, :].bitcast(FP8X4), scales=w_scales[:, j, :], in_=w_grouped[:])
+            bias_bank = sums.tile([P, E], BF16, tag="sums")
+            nc.tensor.matmul(out=bias_bank[:], lhsT=ones[:], rhs=bias_rows[:, j, :], start=True, stop=True)
+            nc.scalar.copy(out=bias_all[:, j, :], in_=bias_bank[:])
+
+        made = {}
+
+        def statistics(n):
+            stats = small.tile([P, GROUP, 6], F32)
+            mean_var = small.tile([P, GROUP, 2], F32)
+            for i in range(GROUP):
+                nc.vector.bn_stats(out=stats[:, i, :], in_=x_sb[stream_of(n)][:, tiles_of(n), :][:, i, :])
+            for i in range(GROUP):
+                nc.vector.bn_aggr(out=mean_var[:, i, :], in_=stats[:, i, :])
+            made["mean_var", n] = mean_var
+
+        def standard_deviation(n):
+            std = small.tile([P, GROUP], F32)
+            nc.scalar.activation(out=std[:], in_=made["mean_var", n][:, :, 1], func=ACT.Sqrt, bias=eps[:], scale=1.0)
+            made["std", n] = std
+
+        def scale_and_offset(n):
+            rstd = small.tile([P, GROUP], F32)
+            nc.vector.reciprocal(out=rstd[:], in_=made["std", n][:])
+            offset = small.tile([P, GROUP], F32)
+            nc.vector.scalar_tensor_tensor(
+                out=offset[:], in0=made["mean_var", n][:, :, 0], scalar=-1.0, in1=rstd[:], op0=ALU.mult, op1=ALU.mult
+            )
+            made["rstd", n] = rstd
+            made["offset", n] = offset
+
+        def normalise(n):
+            x_hat = work.tile([P, GROUP, D], F32)
+            x = x_sb[stream_of(n)][:, tiles_of(n), :]
+            rstd, offset = made["rstd", n], made["offset", n]
+            nc.scalar.activation(
+                out=x_hat[:, 0, :].rearrange("p (u e q) -> p u e q", u=2, e=2),
+                in_=x[:, 0, :].rearrange("p (u q e) -> p u e q", u=2, e=2),
+                func=ACT.Identity,
+                scale=rstd[:, 0:1],
+                bias=offset[:, 0:1],
+            )
+            nc.gpsimd.tensor_scalar(
+                out=x_hat[:, 1, :].rearrange("p (u e q) -> p u e q", u=2, e=2),
+                in0=x[:, 1, :].rearrange("p (u q e) -> p u e q", u=2, e=2),
+                scalar1=rstd[:, 1:2],
+                scalar2=offset[:, 1:2],
+                op0=ALU.mult,
+                op1=ALU.add,
+            )
+            made["x_hat", n] = x_hat
+
+        def transpose_tokens(n):
+            banks = [flip.tile([P, 2, TOKENS], F32, name="x_hat_t%d" % u, tag="flip") for u in range(2)]
+            for i in range(GROUP):
+                for t in range(PACK):
+                    nc.tensor.transpose(
+                        banks[t // 2][:, t % 2, i * P : (i + 1) * P], made["x_hat", n][:, i, t * P : (t + 1) * P], ident[:]
+                    )
+            made["banks", n] = banks
+
+        def gain_and_shift(n):
+            planes = work.tile([P, PACK, TOKENS], BF16)
+            first = 2 * PACK * stream_of(n)
+            for t in range(PACK):
+                nc.scalar.activation(
+                    out=planes[:, t, :],
+                    in_=made["banks", n][t // 2][:, t % 2, :],
+                    func=ACT.Identity,
+                    scale=ln_cols[:, first + t : first + t + 1],
+                    bias=ln_cols[:, first + PACK + t : first + PACK + t + 1],
+                )
+            made["planes", n] = planes
+
+        def regroup(n):
+            grouped = work.tile([P, TOKENS, PACK], BF16, align_bytes=64)
+            nc.vector.tensor_copy(
+                out=grouped[:].rearrange("p (c m) t -> p c t m", m=4),
+                in_=made["planes", n][:].rearrange("p t (c m) -> p c t m", m=4),
+            )
+            made["grouped", n] = grouped
+
+        def quantise(n):
+            codes = work.tile([P, TOKENS], U32, align_bytes=64)
+            scales = work.tile([P, TOKENS], U8, align_bytes=64)
+            nc.vector.quantize_mx(
+                out=codes[:].bitcast(FP8X4), scales=scales[:], in_=made["grouped", n][:].rearrange("p c t -> p (c t)")
+            )
+            made["codes", n] = codes
+            made["scales", n] = scales
+
+        def project(n):
+            s = stream_of(n)
+            result = results.tile([P, 3, GROUP, E], F32)
+            for o in (2, 0, 1):
+                j = qkv_of_stream[s][o]
+                for i in range(GROUP):
+                    tokens = slice(i * P, (i + 1) * P)
+                    bank = sums.tile([P, E], F32, tag="sums")
+                    nc.tensor.matmul_mx(
+                        out=bank[:],
+                        lhsT=made["codes", n][:, tokens].bitcast(FP8X4),
+                        lhsT_scale=made["scales", n][:, tokens],
+                        rhs=w_codes[:, j, :].bitcast(FP8X4),
+                        rhs_scale=w_scales[:, j, :],
+                        start=True,
+                        stop=True,
+                    )
+                    if o == 2:
+                        nc.scalar.copy(out=result[:, o, i, :], in_=bank[:])
+                        nc.gpsimd.tensor_tensor(out=result[:, o, i, :], in0=result[:, o, i, :], in1=bias_all[:, j, :], op=ALU.add)
+                    else:
+                        nc.vector.tensor_tensor(out=result[:, o, i, :], in0=bank[:], in1=bias_all[:, j, :], op=ALU.add)
+            for o in (0, 1, 2):
+                nc.sync.dma_start(out=out_dram[o][s, :, tiles_of(n), :], in_=result[:, o, :, :])
+
+        def in_range(n):
+            return 0 <= n < GROUPS
+
+        for n in range(-STATS_AHEAD, GROUPS):
+            if n == -2:
+                spread_layer_norm_vectors()
+            if in_range(n + 1):
+                gain_and_shift(n + 1)
+            if in_range(n + 2):
+                normalise(n + 2)
+            if in_range(n + 3):
+                standard_deviation(n + 3)
+            if in_range(n + 1):
+                regroup(n + 1)
+            if in_range(n + 3):
+                scale_and_offset(n + 3)
+            if in_range(n + STATS_AHEAD):
+                statistics(n + STATS_AHEAD)
+            if in_range(n + 1):
+                quantise(n + 1)
+            if 0 <= n + 3 < 5:
+                prepare_weight(n + 3)
+            if in_range(n):
+                project(n)
+            if in_range(n + 2):
+                transpose_tokens(n + 2)

@@ -149,13 +149,12 @@ def tile_modalityadaptivemodule_pa_kernel(
                 scale=rstd[:, 0:1],
                 bias=offset[:, 0:1],
             )
-            nc.gpsimd.tensor_scalar(
+            nc.scalar.activation(
                 out=x_hat[:, 1, :].rearrange("p (u e q) -> p u e q", u=2, e=2),
-                in0=x[:, 1, :].rearrange("p (u q e) -> p u e q", u=2, e=2),
-                scalar1=rstd[:, 1:2],
-                scalar2=offset[:, 1:2],
-                op0=ALU.mult,
-                op1=ALU.add,
+                in_=x[:, 1, :].rearrange("p (u q e) -> p u e q", u=2, e=2),
+                func=ACT.Identity,
+                scale=rstd[:, 1:2],
+                bias=offset[:, 1:2],
             )
             made["x_hat", n] = x_hat
 
@@ -201,7 +200,7 @@ def tile_modalityadaptivemodule_pa_kernel(
         def project(n):
             s = stream_of(n)
             result = results.tile([P, 3, GROUP, E], F32)
-            for o in (2, 0, 1):
+            for o in range(3):
                 j = qkv_of_stream[s][o]
                 for i in range(GROUP):
                     tokens = slice(i * P, (i + 1) * P)
@@ -215,11 +214,7 @@ def tile_modalityadaptivemodule_pa_kernel(
                         start=True,
                         stop=True,
                     )
-                    if o == 2:
-                        nc.scalar.copy(out=result[:, o, i, :], in_=bank[:])
-                        nc.gpsimd.tensor_tensor(out=result[:, o, i, :], in0=result[:, o, i, :], in1=bias_all[:, j, :], op=ALU.add)
-                    else:
-                        nc.vector.tensor_tensor(out=result[:, o, i, :], in0=bank[:], in1=bias_all[:, j, :], op=ALU.add)
+                    nc.vector.tensor_tensor(out=result[:, o, i, :], in0=bank[:], in1=bias_all[:, j, :], op=ALU.add)
             for o in (0, 1, 2):
                 nc.sync.dma_start(out=out_dram[o][s, :, tiles_of(n), :], in_=result[:, o, :, :])
 

@@ -19,6 +19,7 @@ TILES = 8
 GROUP = 2
 GROUPS = 2 * TILES // GROUP
 TOKENS = GROUP * P
+V_SHARE = 1
 STATS_AHEAD = 6
 EPS = 1e-5
 
@@ -47,10 +48,9 @@ def tile_modalityadaptivemodule_pa_kernel(
         return slice(first, first + GROUP)
 
     with ExitStack() as ctx:
-        ctx.enter_context(tc.manual_schedule())
         keep = ctx.enter_context(tc.tile_pool(name="keep", bufs=1))
         small = ctx.enter_context(tc.tile_pool(name="small", bufs=STATS_AHEAD))
-        work = ctx.enter_context(tc.tile_pool(name="work", bufs=2))
+        work = ctx.enter_context(tc.tile_pool(name="work", bufs=3))
         results = ctx.enter_context(tc.tile_pool(name="results", bufs=4))
         flip = ctx.enter_context(tc.psum_pool(name="flip", bufs=2))
         sums = ctx.enter_context(tc.psum_pool(name="sums", bufs=6))
@@ -101,7 +101,7 @@ def tile_modalityadaptivemodule_pa_kernel(
             w_grouped = work.tile([P, E * PACK], BF16, align_bytes=64)
             w_words = w_grouped[:].bitcast(F32).rearrange("p (r u) -> p r u", u=2)
             for half in range(2):
-                bank = flip.tile([P, 2, 2 * P], F32, tag="flip")
+                bank = sums.tile([P, 2, 2 * P], F32, tag="sums")
                 for c in range(2):
                     rows_as_words = w_sb[j][:, 2 * half + c, :].bitcast(F32)
                     for u in range(2):
@@ -123,18 +123,17 @@ def tile_modalityadaptivemodule_pa_kernel(
                 nc.vector.bn_aggr(out=mean_var[:, i, :], in_=stats[:, i, :])
             made["mean_var", n] = mean_var
 
-        def standard_deviation(n):
-            std = small.tile([P, GROUP], F32)
-            nc.scalar.activation(out=std[:], in_=made["mean_var", n][:, :, 1], func=ACT.Sqrt, bias=eps[:], scale=1.0)
-            made["std", n] = std
-
         def scale_and_offset(n):
+            mean_var = made["mean_var", n]
+            std = small.tile([P, GROUP], F32)
+            nc.scalar.activation(out=std[:], in_=mean_var[:, :, 1], func=ACT.Sqrt, bias=eps[:], scale=1.0)
             rstd = small.tile([P, GROUP], F32)
-            nc.vector.reciprocal(out=rstd[:], in_=made["std", n][:])
+            nc.vector.reciprocal(out=rstd[:], in_=std[:])
+            minus_rstd = small.tile([P, GROUP], F32)
+            nc.scalar.mul(out=minus_rstd[:], in_=rstd[:], mul=-1.0)
             offset = small.tile([P, GROUP], F32)
-            nc.vector.scalar_tensor_tensor(
-                out=offset[:], in0=made["mean_var", n][:, :, 0], scalar=-1.0, in1=rstd[:], op0=ALU.mult, op1=ALU.mult
-            )
+            for i in range(GROUP):
+                nc.scalar.activation(out=offset[:, i : i + 1], in_=mean_var[:, i, 0:1], func=ACT.Copy, scale=minus_rstd[:, i : i + 1])
             made["rstd", n] = rstd
             made["offset", n] = offset
 
@@ -142,20 +141,15 @@ def tile_modalityadaptivemodule_pa_kernel(
             x_hat = work.tile([P, GROUP, D], F32)
             x = x_sb[stream_of(n)][:, tiles_of(n), :]
             rstd, offset = made["rstd", n], made["offset", n]
-            nc.scalar.activation(
-                out=x_hat[:, 0, :].rearrange("p (u e q) -> p u e q", u=2, e=2),
-                in_=x[:, 0, :].rearrange("p (u q e) -> p u e q", u=2, e=2),
-                func=ACT.Identity,
-                scale=rstd[:, 0:1],
-                bias=offset[:, 0:1],
-            )
-            nc.scalar.activation(
-                out=x_hat[:, 1, :].rearrange("p (u e q) -> p u e q", u=2, e=2),
-                in_=x[:, 1, :].rearrange("p (u q e) -> p u e q", u=2, e=2),
-                func=ACT.Identity,
-                scale=rstd[:, 1:2],
-                bias=offset[:, 1:2],
-            )
+            for i in range(GROUP):
+                nc.gpsimd.tensor_scalar(
+                    out=x_hat[:, i, :].rearrange("p (u e q) -> p u e q", u=2, e=2),
+                    in0=x[:, i, :].rearrange("p (u q e) -> p u e q", u=2, e=2),
+                    scalar1=rstd[:, i : i + 1],
+                    scalar2=offset[:, i : i + 1],
+                    op0=ALU.mult,
+                    op1=ALU.add,
+                )
             made["x_hat", n] = x_hat
 
         def transpose_tokens(n):
@@ -182,7 +176,7 @@ def tile_modalityadaptivemodule_pa_kernel(
 
         def regroup(n):
             grouped = work.tile([P, TOKENS, PACK], BF16, align_bytes=64)
-            nc.vector.tensor_copy(
+            nc.scalar.copy(
                 out=grouped[:].rearrange("p (c m) t -> p c t m", m=4),
                 in_=made["planes", n][:].rearrange("p t (c m) -> p c t m", m=4),
             )
@@ -200,7 +194,7 @@ def tile_modalityadaptivemodule_pa_kernel(
         def project(n):
             s = stream_of(n)
             result = results.tile([P, 3, GROUP, E], F32)
-            for o in range(3):
+            for o in (2, 0, 1):
                 j = qkv_of_stream[s][o]
                 for i in range(GROUP):
                     tokens = slice(i * P, (i + 1) * P)
@@ -214,7 +208,11 @@ def tile_modalityadaptivemodule_pa_kernel(
                         start=True,
                         stop=True,
                     )
-                    nc.vector.tensor_tensor(out=result[:, o, i, :], in0=bank[:], in1=bias_all[:, j, :], op=ALU.add)
+                    if o == 2 and i >= GROUP - V_SHARE:
+                        nc.scalar.copy(out=result[:, o, i, :], in_=bank[:])
+                        nc.gpsimd.tensor_tensor(out=result[:, o, i, :], in0=result[:, o, i, :], in1=bias_all[:, j, :], op=ALU.add)
+                    else:
+                        nc.vector.tensor_tensor(out=result[:, o, i, :], in0=bank[:], in1=bias_all[:, j, :], op=ALU.add)
             for o in (0, 1, 2):
                 nc.sync.dma_start(out=out_dram[o][s, :, tiles_of(n), :], in_=result[:, o, :, :])
 
@@ -226,14 +224,11 @@ def tile_modalityadaptivemodule_pa_kernel(
                 spread_layer_norm_vectors()
             if in_range(n + 1):
                 gain_and_shift(n + 1)
-            if in_range(n + 2):
-                normalise(n + 2)
-            if in_range(n + 3):
-                standard_deviation(n + 3)
-            if in_range(n + 1):
                 regroup(n + 1)
             if in_range(n + 3):
                 scale_and_offset(n + 3)
+            if in_range(n + 2):
+                normalise(n + 2)
             if in_range(n + STATS_AHEAD):
                 statistics(n + STATS_AHEAD)
             if in_range(n + 1):

@@ -214,7 +214,8 @@ def tile_modalityadaptivemodule_pa_kernel(
                     else:
                         nc.vector.tensor_tensor(out=result[:, o, i, :], in0=bank[:], in1=bias_all[:, j, :], op=ALU.add)
             for o in (0, 1, 2):
-                nc.sync.dma_start(out=out_dram[o][s, :, tiles_of(n), :], in_=result[:, o, :, :])
+                for i in range(GROUP):
+                    nc.sync.dma_start(out=out_dram[o][s, :, tiles_of(n), :][:, i, :], in_=result[:, o, i, :])
 
         def in_range(n):
             return 0 <= n < GROUPS

@@ -19,7 +19,6 @@ TILES = 8
 GROUP = 2
 GROUPS = 2 * TILES // GROUP
 TOKENS = GROUP * P
-V_SHARE = 1
 STATS_AHEAD = 6
 EPS = 1e-5
 
@@ -194,7 +193,7 @@ def tile_modalityadaptivemodule_pa_kernel(
         def project(n):
             s = stream_of(n)
             result = results.tile([P, 3, GROUP, E], F32)
-            for o in (2, 0, 1):
+            for o in range(3):
                 j = qkv_of_stream[s][o]
                 for i in range(GROUP):
                     tokens = slice(i * P, (i + 1) * P)
@@ -208,14 +207,9 @@ def tile_modalityadaptivemodule_pa_kernel(
                         start=True,
                         stop=True,
                     )
-                    if o == 2 and i >= GROUP - V_SHARE:
-                        nc.scalar.copy(out=result[:, o, i, :], in_=bank[:])
-                        nc.gpsimd.tensor_tensor(out=result[:, o, i, :], in0=result[:, o, i, :], in1=bias_all[:, j, :], op=ALU.add)
-                    else:
-                        nc.vector.tensor_tensor(out=result[:, o, i, :], in0=bank[:], in1=bias_all[:, j, :], op=ALU.add)
+                    nc.vector.tensor_tensor(out=result[:, o, i, :], in0=bank[:], in1=bias_all[:, j, :], op=ALU.add)
             for o in (0, 1, 2):
-                for i in range(GROUP):
-                    nc.sync.dma_start(out=out_dram[o][s, :, tiles_of(n), :][:, i, :], in_=result[:, o, i, :])
+                nc.sync.dma_start(out=out_dram[o][s, :, tiles_of(n), :], in_=result[:, o, :, :])
 
         def in_range(n):
             return 0 <= n < GROUPS

@@ -19,7 +19,6 @@ TILES = 8
 GROUP = 2
 GROUPS = 2 * TILES // GROUP
 TOKENS = GROUP * P
-STATS_AHEAD = 6
 EPS = 1e-5
 
 FLOPS = 2 * 2 * TILES * P * D * 3 * E
@@ -48,9 +47,9 @@ def tile_modalityadaptivemodule_pa_kernel(
 
     with ExitStack() as ctx:
         keep = ctx.enter_context(tc.tile_pool(name="keep", bufs=1))
-        small = ctx.enter_context(tc.tile_pool(name="small", bufs=STATS_AHEAD))
-        work = ctx.enter_context(tc.tile_pool(name="work", bufs=3))
-        results = ctx.enter_context(tc.tile_pool(name="results", bufs=4))
+        small = ctx.enter_context(tc.tile_pool(name="small", bufs=GROUPS))
+        work = ctx.enter_context(tc.tile_pool(name="work", bufs=4))
+        results = ctx.enter_context(tc.tile_pool(name="results", bufs=6))
         flip = ctx.enter_context(tc.psum_pool(name="flip", bufs=2))
         sums = ctx.enter_context(tc.psum_pool(name="sums", bufs=6))
 
@@ -58,10 +57,10 @@ def tile_modalityadaptivemodule_pa_kernel(
         make_identity(nc, ident[:])
         ln_rows = keep.tile([P, D // 2], BF16)
         nc.vector.memset(ln_rows[:], 0.0)
-        bias_rows = keep.tile([P, 5, E], BF16)
+        bias_rows = keep.tile([P, E], BF16)
         nc.vector.memset(bias_rows[:], 0.0)
-        ones = keep.tile([P, P], BF16)
-        nc.vector.memset(ones[:], 1.0)
+        pick = keep.tile([P, 5], BF16)
+        nc.vector.tensor_copy(out=pick[:], in_=ident[:, 0:5])
         eps = keep.tile([P, 1], F32)
         nc.vector.memset(eps[:], EPS)
 
@@ -75,14 +74,25 @@ def tile_modalityadaptivemodule_pa_kernel(
         def load_weight(j):
             nc.sync.dma_start(out=w_sb[j][:], in_=weights[j].rearrange("(c p) d -> p c d", p=P))
 
-        for v in range(4):
-            nc.scalar.dma_start(out=ln_rows[2 * v : 2 * v + 2, :], in_=ln_vectors[v].rearrange("(u w) -> u w", u=2))
+        def load_bias(j):
+            nc.sync.dma_start(out=bias_rows[j : j + 1, :], in_=biases[j].rearrange("(o e) -> o e", o=1))
+
         load_tokens(0)
+        for v in range(4):
+            nc.sync.dma_start(out=ln_rows[2 * v : 2 * v + 2, :], in_=ln_vectors[v].rearrange("(u w) -> u w", u=2))
+        load_weight(0)
         load_tokens(1)
         for j in range(5):
-            load_weight(j)
-            nc.sync.dma_start(out=bias_rows[0:1, j, :], in_=biases[j].rearrange("(o e) -> o e", o=1))
-            load_tokens(j + 2)
+            load_bias(j)
+        load_weight(1)
+        load_tokens(2)
+        load_weight(2)
+        load_tokens(3)
+        load_tokens(4)
+        load_weight(3)
+        load_tokens(5)
+        load_weight(4)
+        load_tokens(6)
         load_tokens(7)
 
         ln_cols = keep.tile([P, 4 * PACK], F32)
@@ -95,23 +105,34 @@ def tile_modalityadaptivemodule_pa_kernel(
         w_codes = keep.tile([P, 5, E], U32, align_bytes=64)
         w_scales = keep.tile([P, 5, E], U8, align_bytes=64)
         bias_all = keep.tile([P, 5, E], BF16)
+        made = {}
 
-        def prepare_weight(j):
-            w_grouped = work.tile([P, E * PACK], BF16, align_bytes=64)
-            w_words = w_grouped[:].bitcast(F32).rearrange("p (r u) -> p r u", u=2)
+        def transpose_weight(j):
             for half in range(2):
                 bank = sums.tile([P, 2, 2 * P], F32, tag="sums")
                 for c in range(2):
                     rows_as_words = w_sb[j][:, 2 * half + c, :].bitcast(F32)
                     for u in range(2):
                         nc.tensor.transpose(bank[:, u, c * P : (c + 1) * P], rows_as_words[:, u * P : (u + 1) * P], ident[:])
-                nc.scalar.copy(out=w_words[:, half * 2 * P : (half + 1) * 2 * P, :], in_=bank[:].rearrange("p u r -> p r u"))
-            nc.vector.quantize_mx(out=w_codes[:, j, :].bitcast(FP8X4), scales=w_scales[:, j, :], in_=w_grouped[:])
-            bias_bank = sums.tile([P, E], BF16, tag="sums")
-            nc.tensor.matmul(out=bias_bank[:], lhsT=ones[:], rhs=bias_rows[:, j, :], start=True, stop=True)
-            nc.scalar.copy(out=bias_all[:, j, :], in_=bias_bank[:])
+                made["w_bank", j, half] = bank
 
-        made = {}
+        def copy_weight(j):
+            w_grouped = work.tile([P, E * PACK], BF16, align_bytes=64)
+            w_words = w_grouped[:].bitcast(F32).rearrange("p (r u) -> p r u", u=2)
+            for half in range(2):
+                nc.scalar.copy(
+                    out=w_words[:, half * 2 * P : (half + 1) * 2 * P, :],
+                    in_=made["w_bank", j, half][:].rearrange("p u r -> p r u"),
+                )
+            made["w_grouped", j] = w_grouped
+
+        def quantise_weight(j):
+            nc.vector.quantize_mx(out=w_codes[:, j, :].bitcast(FP8X4), scales=w_scales[:, j, :], in_=made["w_grouped", j][:])
+
+        def spread_bias(j):
+            bias_bank = sums.tile([P, E], BF16, tag="sums")
+            nc.tensor.matmul(out=bias_bank[:], lhsT=pick[:, j : j + 1].to_broadcast([P, P]), rhs=bias_rows[:], start=True, stop=True)
+            nc.scalar.copy(out=bias_all[:, j, :], in_=bias_bank[:])
 
         def statistics(n):
             stats = small.tile([P, GROUP, 6], F32)
@@ -122,32 +143,29 @@ def tile_modalityadaptivemodule_pa_kernel(
                 nc.vector.bn_aggr(out=mean_var[:, i, :], in_=stats[:, i, :])
             made["mean_var", n] = mean_var
 
-        def scale_and_offset(n):
+        def std_and_mean(n):
             mean_var = made["mean_var", n]
             std = small.tile([P, GROUP], F32)
             nc.scalar.activation(out=std[:], in_=mean_var[:, :, 1], func=ACT.Sqrt, bias=eps[:], scale=1.0)
-            rstd = small.tile([P, GROUP], F32)
-            nc.vector.reciprocal(out=rstd[:], in_=std[:])
-            minus_rstd = small.tile([P, GROUP], F32)
-            nc.scalar.mul(out=minus_rstd[:], in_=rstd[:], mul=-1.0)
-            offset = small.tile([P, GROUP], F32)
-            for i in range(GROUP):
-                nc.scalar.activation(out=offset[:, i : i + 1], in_=mean_var[:, i, 0:1], func=ACT.Copy, scale=minus_rstd[:, i : i + 1])
-            made["rstd", n] = rstd
-            made["offset", n] = offset
+            minus_mean = small.tile([P, GROUP], F32)
+            nc.scalar.mul(out=minus_mean[:], in_=mean_var[:, :, 0], mul=-1.0)
+            made["std", n] = std
+            made["offset", n] = minus_mean
 
         def normalise(n):
+            rstd = small.tile([P, GROUP], F32)
+            nc.vector.reciprocal(out=rstd[:], in_=made["std", n][:])
             x_hat = work.tile([P, GROUP, D], F32)
             x = x_sb[stream_of(n)][:, tiles_of(n), :]
-            rstd, offset = made["rstd", n], made["offset", n]
+            offset = made["offset", n]
             for i in range(GROUP):
                 nc.gpsimd.tensor_scalar(
                     out=x_hat[:, i, :].rearrange("p (u e q) -> p u e q", u=2, e=2),
                     in0=x[:, i, :].rearrange("p (u q e) -> p u e q", u=2, e=2),
-                    scalar1=rstd[:, i : i + 1],
-                    scalar2=offset[:, i : i + 1],
-                    op0=ALU.mult,
-                    op1=ALU.add,
+                    scalar1=offset[:, i : i + 1],
+                    scalar2=rstd[:, i : i + 1],
+                    op0=ALU.add,
+                    op1=ALU.mult,
                 )
             made["x_hat", n] = x_hat
 
@@ -190,47 +208,150 @@ def tile_modalityadaptivemodule_pa_kernel(
             made["codes", n] = codes
             made["scales", n] = scales
 
-        def project(n):
+        def project(n, o):
             s = stream_of(n)
-            result = results.tile([P, 3, GROUP, E], F32)
-            for o in range(3):
-                j = qkv_of_stream[s][o]
-                for i in range(GROUP):
-                    tokens = slice(i * P, (i + 1) * P)
-                    bank = sums.tile([P, E], F32, tag="sums")
-                    nc.tensor.matmul_mx(
-                        out=bank[:],
-                        lhsT=made["codes", n][:, tokens].bitcast(FP8X4),
-                        lhsT_scale=made["scales", n][:, tokens],
-                        rhs=w_codes[:, j, :].bitcast(FP8X4),
-                        rhs_scale=w_scales[:, j, :],
-                        start=True,
-                        stop=True,
-                    )
-                    nc.vector.tensor_tensor(out=result[:, o, i, :], in0=bank[:], in1=bias_all[:, j, :], op=ALU.add)
-            for o in (0, 1, 2):
-                nc.sync.dma_start(out=out_dram[o][s, :, tiles_of(n), :], in_=result[:, o, :, :])
+            j = qkv_of_stream[s][o]
+            result = results.tile([P, GROUP, E], F32)
+            for i in range(GROUP):
+                tokens = slice(i * P, (i + 1) * P)
+                bank = sums.tile([P, E], F32, tag="sums")
+                nc.tensor.matmul_mx(
+                    out=bank[:],
+                    lhsT=made["codes", n][:, tokens].bitcast(FP8X4),
+                    lhsT_scale=made["scales", n][:, tokens],
+                    rhs=w_codes[:, j, :].bitcast(FP8X4),
+                    rhs_scale=w_scales[:, j, :],
+                    start=True,
+                    stop=True,
+                )
+                nc.vector.tensor_tensor(out=result[:, i, :], in0=bank[:], in1=bias_all[:, j, :], op=ALU.add)
+            made["result", n, o] = result
 
-        def in_range(n):
-            return 0 <= n < GROUPS
+        def store(n, o):
+            nc.sync.dma_start(out=out_dram[o][stream_of(n), :, tiles_of(n), :], in_=made["result", n, o][:])
 
-        for n in range(-STATS_AHEAD, GROUPS):
-            if n == -2:
-                spread_layer_norm_vectors()
-            if in_range(n + 1):
-                gain_and_shift(n + 1)
-                regroup(n + 1)
-            if in_range(n + 3):
-                scale_and_offset(n + 3)
-            if in_range(n + 2):
-                normalise(n + 2)
-            if in_range(n + STATS_AHEAD):
-                statistics(n + STATS_AHEAD)
-            if in_range(n + 1):
-                quantise(n + 1)
-            if 0 <= n + 3 < 5:
-                prepare_weight(n + 3)
-            if in_range(n):
-                project(n)
-            if in_range(n + 2):
-                transpose_tokens(n + 2)
+        spread_layer_norm_vectors()
+        statistics(0)
+        std_and_mean(0)
+        normalise(0)
+        transpose_weight(0)
+        copy_weight(0)
+        quantise_weight(0)
+        spread_bias(0)
+        statistics(1)
+        std_and_mean(1)
+        normalise(1)
+        transpose_weight(1)
+        copy_weight(1)
+        quantise_weight(1)
+        spread_bias(1)
+        statistics(2)
+        std_and_mean(2)
+        normalise(2)
+        transpose_tokens(0)
+        gain_and_shift(0)
+        regroup(0)
+        quantise(0)
+        transpose_weight(2)
+        copy_weight(2)
+        quantise_weight(2)
+        spread_bias(2)
+        statistics(3)
+        std_and_mean(3)
+        normalise(3)
+        transpose_tokens(1)
+        gain_and_shift(1)
+        regroup(1)
+        quantise(1)
+        transpose_weight(3)
+        copy_weight(3)
+        quantise_weight(3)
+        spread_bias(3)
+        project(0, 0)
+        store(0, 0)
+        project(0, 1)
+        store(0, 1)
+        project(0, 2)
+        store(0, 2)
+        statistics(4)
+        std_and_mean(4)
+        normalise(4)
+        transpose_tokens(2)
+        gain_and_shift(2)
+        regroup(2)
+        quantise(2)
+        transpose_weight(4)
+        copy_weight(4)
+        quantise_weight(4)
+        spread_bias(4)
+        project(1, 0)
+        store(1, 0)
+        project(1, 1)
+        store(1, 1)
+        project(1, 2)
+        store(1, 2)
+        statistics(5)
+        std_and_mean(5)
+        normalise(5)
+        transpose_tokens(3)
+        gain_and_shift(3)
+        regroup(3)
+        quantise(3)
+        project(2, 0)
+        store(2, 0)
+        project(2, 1)
+        store(2, 1)
+        project(2, 2)
+        store(2, 2)
+        statistics(6)
+        std_and_mean(6)
+        normalise(6)
+        transpose_tokens(4)
+        gain_and_shift(4)
+        regroup(4)
+        quantise(4)
+        project(3, 0)
+        store(3, 0)
+        project(3, 1)
+        store(3, 1)
+        project(3, 2)
+        store(3, 2)
+        statistics(7)
+        std_and_mean(7)
+        normalise(7)
+        transpose_tokens(5)
+        gain_and_shift(5)
+        regroup(5)
+        quantise(5)
+        project(4, 0)
+        store(4, 0)
+        project(4, 1)
+        store(4, 1)
+        project(4, 2)
+        store(4, 2)
+        transpose_tokens(6)
+        gain_and_shift(6)
+        regroup(6)
+        quantise(6)
+        project(5, 0)
+        store(5, 0)
+        project(5, 1)
+        store(5, 1)
+        project(5, 2)
+        store(5, 2)
+        transpose_tokens(7)
+        gain_and_shift(7)
+        regroup(7)
+        quantise(7)
+        project(6, 0)
+        store(6, 0)
+        project(6, 1)
+        store(6, 1)
+        project(6, 2)
+        store(6, 2)
+        project(7, 0)
+        store(7, 0)
+        project(7, 1)
+        store(7, 1)
+        project(7, 2)
+        store(7, 2)

@@ -72,7 +72,7 @@ def tile_modalityadaptivemodule_pa_kernel(
             nc.sync.dma_start(out=x_sb[s][:, tiles_of(n), :], in_=x_dram[s][:, tiles_of(n), :])
 
         def load_weight(j):
-            nc.sync.dma_start(out=w_sb[j][:], in_=weights[j].rearrange("(c p) d -> p c d", p=P))
+            nc.sync.dma_start(out=w_sb[j][:], in_=weights[j].rearrange("(p c) d -> p c d", p=P))
 
         def load_bias(j):
             nc.sync.dma_start(out=bias_rows[j : j + 1, :], in_=biases[j].rearrange("(o e) -> o e", o=1))
@@ -118,11 +118,11 @@ def tile_modalityadaptivemodule_pa_kernel(
 
         def copy_weight(j):
             w_grouped = work.tile([P, E * PACK], BF16, align_bytes=64)
-            w_words = w_grouped[:].bitcast(F32).rearrange("p (r u) -> p r u", u=2)
+            w_words = w_grouped[:].bitcast(F32).rearrange("i (p c u) -> i p c u", c=4, u=2)
             for half in range(2):
                 nc.scalar.copy(
-                    out=w_words[:, half * 2 * P : (half + 1) * 2 * P, :],
-                    in_=made["w_bank", j, half][:].rearrange("p u r -> p r u"),
+                    out=w_words[:, :, 2 * half : 2 * half + 2, :],
+                    in_=made["w_bank", j, half][:].rearrange("i u (c p) -> i p c u", p=P),
                 )
             made["w_grouped", j] = w_grouped
 

@@ -49,7 +49,7 @@ def tile_modalityadaptivemodule_pa_kernel(
         keep = ctx.enter_context(tc.tile_pool(name="keep", bufs=1))
         small = ctx.enter_context(tc.tile_pool(name="small", bufs=GROUPS))
         work = ctx.enter_context(tc.tile_pool(name="work", bufs=4))
-        results = ctx.enter_context(tc.tile_pool(name="results", bufs=6))
+        results = ctx.enter_context(tc.tile_pool(name="results", bufs=10))
         flip = ctx.enter_context(tc.psum_pool(name="flip", bufs=2))
         sums = ctx.enter_context(tc.psum_pool(name="sums", bufs=6))
 
@@ -95,17 +95,21 @@ def tile_modalityadaptivemodule_pa_kernel(
         load_tokens(6)
         load_tokens(7)
 
+        made = {}
+
         ln_cols = keep.tile([P, 4 * PACK], F32)
 
-        def spread_layer_norm_vectors():
+        def transpose_layer_norm_vectors():
             ln_bank = flip.tile([P, P], F32, tag="flip")
             nc.tensor.transpose(ln_bank[:], ln_rows[:].bitcast(F32), ident[:])
-            nc.scalar.copy(out=ln_cols[:], in_=ln_bank[:, 0:8].bitcast(BF16))
+            made["ln_bank"] = ln_bank
+
+        def copy_layer_norm_vectors():
+            nc.scalar.copy(out=ln_cols[:], in_=made["ln_bank"][:, 0:8].bitcast(BF16))
 
         w_codes = keep.tile([P, 5, E], U32, align_bytes=64)
         w_scales = keep.tile([P, 5, E], U8, align_bytes=64)
         bias_all = keep.tile([P, 5, E], BF16)
-        made = {}
 
         def transpose_weight(j):
             for half in range(2):
@@ -132,29 +136,50 @@ def tile_modalityadaptivemodule_pa_kernel(
         def spread_bias(j):
             bias_bank = sums.tile([P, E], BF16, tag="sums")
             nc.tensor.matmul(out=bias_bank[:], lhsT=pick[:, j : j + 1].to_broadcast([P, P]), rhs=bias_rows[:], start=True, stop=True)
-            nc.scalar.copy(out=bias_all[:, j, :], in_=bias_bank[:])
+            made["bias_bank", j] = bias_bank
+
+        def copy_bias(j):
+            nc.scalar.copy(out=bias_all[:, j, :], in_=made["bias_bank", j][:])
 
         def statistics(n):
             stats = small.tile([P, GROUP, 6], F32)
-            mean_var = small.tile([P, GROUP, 2], F32)
             for i in range(GROUP):
                 nc.vector.bn_stats(out=stats[:, i, :], in_=x_sb[stream_of(n)][:, tiles_of(n), :][:, i, :])
+            made["stats", n] = stats
+
+        def aggregate(n):
+            mean_var = small.tile([P, GROUP, 2], F32)
             for i in range(GROUP):
-                nc.vector.bn_aggr(out=mean_var[:, i, :], in_=stats[:, i, :])
+                nc.vector.bn_aggr(out=mean_var[:, i, :], in_=made["stats", n][:, i, :])
             made["mean_var", n] = mean_var
 
-        def std_and_mean(n):
+        def sums_on_scalar(n):
+            minus_mean = small.tile([P, GROUP], F32)
+            x = x_sb[stream_of(n)][:, tiles_of(n), :]
+            total = small.tile([P, GROUP], F32)
+            squares = small.tile([P, GROUP], F32)
+            junk = work.tile([P, D], BF16)
+            for i in range(GROUP):
+                nc.scalar.activation(out=junk[:], in_=x[:, i, :], func=ACT.Copy, accum_out=total[:, i : i + 1])
+            nc.scalar.mul(out=minus_mean[:], in_=total[:], mul=-1.0 / D)
+            for i in range(GROUP):
+                nc.scalar.activation(out=junk[:], in_=x[:, i, :], func=ACT.Square, bias=minus_mean[:, i : i + 1], accum_out=squares[:, i : i + 1])
+            rstd = small.tile([P, GROUP], F32)
+            nc.scalar.activation(out=rstd[:], in_=squares[:], func=ACT.Abs_reciprocal_sqrt, bias=eps[:], scale=1.0 / D)
+            made["rstd", n] = rstd
+            made["offset", n] = minus_mean
+
+        def rstd_and_mean(n):
             mean_var = made["mean_var", n]
-            std = small.tile([P, GROUP], F32)
-            nc.scalar.activation(out=std[:], in_=mean_var[:, :, 1], func=ACT.Sqrt, bias=eps[:], scale=1.0)
+            rstd = small.tile([P, GROUP], F32)
+            nc.scalar.activation(out=rstd[:], in_=mean_var[:, :, 1], func=ACT.Abs_reciprocal_sqrt, bias=eps[:], scale=1.0)
             minus_mean = small.tile([P, GROUP], F32)
             nc.scalar.mul(out=minus_mean[:], in_=mean_var[:, :, 0], mul=-1.0)
-            made["std", n] = std
+            made["rstd", n] = rstd
             made["offset", n] = minus_mean
 
         def normalise(n):
-            rstd = small.tile([P, GROUP], F32)
-            nc.vector.reciprocal(out=rstd[:], in_=made["std", n][:])
+            rstd = made["rstd", n]
             x_hat = work.tile([P, GROUP, D], F32)
             x = x_sb[stream_of(n)][:, tiles_of(n), :]
             offset = made["offset", n]
@@ -208,11 +233,9 @@ def tile_modalityadaptivemodule_pa_kernel(
             made["codes", n] = codes
             made["scales", n] = scales
 
-        def project(n, o):
-            s = stream_of(n)
-            j = qkv_of_stream[s][o]
-            result = results.tile([P, GROUP, E], F32)
+        def multiply(n, o):
             for i in range(GROUP):
+                j = qkv_of_stream[stream_of(n)][o]
                 tokens = slice(i * P, (i + 1) * P)
                 bank = sums.tile([P, E], F32, tag="sums")
                 nc.tensor.matmul_mx(
@@ -224,134 +247,179 @@ def tile_modalityadaptivemodule_pa_kernel(
                     start=True,
                     stop=True,
                 )
-                nc.vector.tensor_tensor(out=result[:, i, :], in0=bank[:], in1=bias_all[:, j, :], op=ALU.add)
+                made["bank", n, o, i] = bank
+
+        def add_bias(n, o):
+            result = results.tile([P, GROUP, E], F32)
+            for i in range(GROUP):
+                j = qkv_of_stream[stream_of(n)][o]
+                nc.vector.tensor_tensor(out=result[:, i, :], in0=made["bank", n, o, i][:], in1=bias_all[:, j, :], op=ALU.add)
             made["result", n, o] = result
 
         def store(n, o):
             nc.sync.dma_start(out=out_dram[o][stream_of(n), :, tiles_of(n), :], in_=made["result", n, o][:])
 
-        spread_layer_norm_vectors()
+        def store_by_tile(n, o):
+            for i in range(GROUP):
+                tile = tiles_of(n).start + i
+                nc.sync.dma_start(out=out_dram[o][stream_of(n), :, tile, :], in_=made["result", n, o][:, i, :])
+
+        transpose_layer_norm_vectors()
+        copy_layer_norm_vectors()
         statistics(0)
-        std_and_mean(0)
+        aggregate(0)
+        rstd_and_mean(0)
         normalise(0)
         transpose_weight(0)
         copy_weight(0)
         quantise_weight(0)
         spread_bias(0)
+        copy_bias(0)
         statistics(1)
-        std_and_mean(1)
+        aggregate(1)
+        rstd_and_mean(1)
         normalise(1)
-        transpose_weight(1)
-        copy_weight(1)
-        quantise_weight(1)
-        spread_bias(1)
-        statistics(2)
-        std_and_mean(2)
-        normalise(2)
         transpose_tokens(0)
         gain_and_shift(0)
         regroup(0)
         quantise(0)
-        transpose_weight(2)
-        copy_weight(2)
-        quantise_weight(2)
-        spread_bias(2)
-        statistics(3)
-        std_and_mean(3)
-        normalise(3)
+        transpose_weight(1)
+        copy_weight(1)
+        quantise_weight(1)
+        spread_bias(1)
+        copy_bias(1)
+        statistics(2)
+        aggregate(2)
+        rstd_and_mean(2)
+        normalise(2)
         transpose_tokens(1)
         gain_and_shift(1)
         regroup(1)
         quantise(1)
-        transpose_weight(3)
-        copy_weight(3)
-        quantise_weight(3)
-        spread_bias(3)
-        project(0, 0)
+        multiply(0, 0)
+        add_bias(0, 0)
         store(0, 0)
-        project(0, 1)
+        transpose_weight(2)
+        copy_weight(2)
+        quantise_weight(2)
+        spread_bias(2)
+        copy_bias(2)
+        statistics(3)
+        aggregate(3)
+        rstd_and_mean(3)
+        normalise(3)
+        multiply(0, 1)
+        add_bias(0, 1)
         store(0, 1)
-        project(0, 2)
-        store(0, 2)
-        statistics(4)
-        std_and_mean(4)
-        normalise(4)
+        multiply(1, 0)
+        add_bias(1, 0)
+        store(1, 0)
+        multiply(1, 1)
+        add_bias(1, 1)
+        store(1, 1)
         transpose_tokens(2)
         gain_and_shift(2)
         regroup(2)
         quantise(2)
-        transpose_weight(4)
-        copy_weight(4)
-        quantise_weight(4)
-        spread_bias(4)
-        project(1, 0)
-        store(1, 0)
-        project(1, 1)
-        store(1, 1)
-        project(1, 2)
+        transpose_weight(3)
+        copy_weight(3)
+        quantise_weight(3)
+        spread_bias(3)
+        copy_bias(3)
+        statistics(4)
+        aggregate(4)
+        rstd_and_mean(4)
+        normalise(4)
+        multiply(0, 2)
+        add_bias(0, 2)
+        store(0, 2)
+        multiply(1, 2)
+        add_bias(1, 2)
         store(1, 2)
-        statistics(5)
-        std_and_mean(5)
-        normalise(5)
         transpose_tokens(3)
         gain_and_shift(3)
         regroup(3)
         quantise(3)
-        project(2, 0)
+        transpose_weight(4)
+        copy_weight(4)
+        quantise_weight(4)
+        spread_bias(4)
+        copy_bias(4)
+        statistics(5)
+        aggregate(5)
+        rstd_and_mean(5)
+        normalise(5)
+        multiply(2, 0)
+        add_bias(2, 0)
         store(2, 0)
-        project(2, 1)
+        multiply(2, 1)
+        add_bias(2, 1)
         store(2, 1)
-        project(2, 2)
+        multiply(2, 2)
+        add_bias(2, 2)
         store(2, 2)
-        statistics(6)
-        std_and_mean(6)
+        sums_on_scalar(6)
         normalise(6)
         transpose_tokens(4)
         gain_and_shift(4)
         regroup(4)
         quantise(4)
-        project(3, 0)
+        multiply(3, 0)
+        add_bias(3, 0)
         store(3, 0)
-        project(3, 1)
+        multiply(3, 1)
+        add_bias(3, 1)
         store(3, 1)
-        project(3, 2)
+        multiply(3, 2)
+        add_bias(3, 2)
         store(3, 2)
-        statistics(7)
-        std_and_mean(7)
+        sums_on_scalar(7)
         normalise(7)
         transpose_tokens(5)
         gain_and_shift(5)
         regroup(5)
         quantise(5)
-        project(4, 0)
+        multiply(4, 0)
+        add_bias(4, 0)
         store(4, 0)
-        project(4, 1)
+        multiply(4, 1)
+        add_bias(4, 1)
         store(4, 1)
-        project(4, 2)
+        multiply(4, 2)
+        add_bias(4, 2)
         store(4, 2)
         transpose_tokens(6)
         gain_and_shift(6)
         regroup(6)
         quantise(6)
-        project(5, 0)
+        multiply(5, 0)
+        add_bias(5, 0)
         store(5, 0)
-        project(5, 1)
+        multiply(5, 1)
+        add_bias(5, 1)
         store(5, 1)
-        project(5, 2)
+        multiply(5, 2)
+        add_bias(5, 2)
         store(5, 2)
         transpose_tokens(7)
         gain_and_shift(7)
         regroup(7)
         quantise(7)
-        project(6, 0)
+        multiply(6, 0)
+        add_bias(6, 0)
         store(6, 0)
-        project(6, 1)
+        multiply(6, 1)
+        add_bias(6, 1)
         store(6, 1)
-        project(6, 2)
+        multiply(6, 2)
+        add_bias(6, 2)
         store(6, 2)
-        project(7, 0)
+        multiply(7, 0)
+        add_bias(7, 0)
         store(7, 0)
-        project(7, 1)
+        multiply(7, 1)
+        add_bias(7, 1)
         store(7, 1)
-        project(7, 2)
+        multiply(7, 2)
+        add_bias(7, 2)
         store(7, 2)

from contextlib import ExitStack

import concourse.mybir as mybir
from concourse.masks import make_identity

F32 = mybir.dt.float32
BF16 = mybir.dt.bfloat16
U32 = mybir.dt.uint32
U8 = mybir.dt.uint8
FP8X4 = mybir.dt.float8_e4m3fn_x4
ACT = mybir.ActivationFunctionType
ALU = mybir.AluOpType

P = 128
PACK = 4
D = P * PACK
E = 512
TILES = 8
GROUP = 2
GROUPS = 2 * TILES // GROUP
TOKENS = GROUP * P
EPS = 1e-5

FLOPS = 2 * 2 * TILES * P * D * 3 * E


def tile_modalityadaptivemodule_pa_kernel(
    tc, text, img, ln_t_g, ln_t_b, ln_i_g, ln_i_b,
    Wq, bq, Wkt, bkt, Wvt, bvt, Wki, bki, Wvi, bvi,
    out_0, out_1, out_2,
):
    nc = tc.nc
    streams = [text, img]
    ln_vectors = [ln_t_g, ln_t_b, ln_i_g, ln_i_b]
    weights = [Wq, Wkt, Wvt, Wki, Wvi]
    biases = [bq, bkt, bvt, bki, bvi]
    qkv_of_stream = [(0, 1, 2), (0, 3, 4)]
    x_dram = [x.flatten_outer_dims().rearrange("(p t) d -> p t d", p=P) for x in streams]
    out_dram = [o.flatten_outer_dims().rearrange("(s p t) e -> s p t e", s=2, p=P) for o in (out_0, out_1, out_2)]

    def stream_of(n):
        return n // (GROUPS // 2)

    def tiles_of(n):
        first = (n % (GROUPS // 2)) * GROUP
        return slice(first, first + GROUP)

    with ExitStack() as ctx:
        keep = ctx.enter_context(tc.tile_pool(name="keep", bufs=1))
        small = ctx.enter_context(tc.tile_pool(name="small", bufs=GROUPS))
        work = ctx.enter_context(tc.tile_pool(name="work", bufs=4))
        results = ctx.enter_context(tc.tile_pool(name="results", bufs=10))
        flip = ctx.enter_context(tc.psum_pool(name="flip", bufs=2))
        sums = ctx.enter_context(tc.psum_pool(name="sums", bufs=6))

        ident = keep.tile([P, P], F32)
        make_identity(nc, ident[:])
        ln_rows = keep.tile([P, D // 2], BF16)
        nc.vector.memset(ln_rows[:], 0.0)
        bias_rows = keep.tile([P, E], BF16)
        nc.vector.memset(bias_rows[:], 0.0)
        pick = keep.tile([P, 5], BF16)
        nc.vector.tensor_copy(out=pick[:], in_=ident[:, 0:5])
        eps = keep.tile([P, 1], F32)
        nc.vector.memset(eps[:], EPS)

        x_sb = [keep.tile([P, TILES, D], BF16, name="x_sb%d" % s) for s in range(2)]
        w_sb = [keep.tile([P, E // P, D], BF16, name="w_sb%d" % j) for j in range(5)]

        def load_tokens(n):
            s = stream_of(n)
            nc.sync.dma_start(out=x_sb[s][:, tiles_of(n), :], in_=x_dram[s][:, tiles_of(n), :])

        def load_weight(j):
            nc.sync.dma_start(out=w_sb[j][:], in_=weights[j].rearrange("(p c) d -> p c d", p=P))

        def load_bias(j):
            nc.sync.dma_start(out=bias_rows[j : j + 1, :], in_=biases[j].rearrange("(o e) -> o e", o=1))

        load_tokens(0)
        for v in range(4):
            nc.sync.dma_start(out=ln_rows[2 * v : 2 * v + 2, :], in_=ln_vectors[v].rearrange("(u w) -> u w", u=2))
        load_weight(0)
        load_tokens(1)
        for j in range(5):
            load_bias(j)
        load_weight(1)
        load_tokens(2)
        load_weight(2)
        load_tokens(3)
        load_tokens(4)
        load_weight(3)
        load_tokens(5)
        load_weight(4)
        load_tokens(6)
        load_tokens(7)

        made = {}

        ln_cols = keep.tile([P, 4 * PACK], F32)

        def transpose_layer_norm_vectors():
            ln_bank = flip.tile([P, P], F32, tag="flip")
            nc.tensor.transpose(ln_bank[:], ln_rows[:].bitcast(F32), ident[:])
            made["ln_bank"] = ln_bank

        def copy_layer_norm_vectors():
            nc.scalar.copy(out=ln_cols[:], in_=made["ln_bank"][:, 0:8].bitcast(BF16))

        w_codes = keep.tile([P, 5, E], U32, align_bytes=64)
        w_scales = keep.tile([P, 5, E], U8, align_bytes=64)
        bias_all = keep.tile([P, 5, E], BF16)

        def transpose_weight(j):
            for half in range(2):
                bank = sums.tile([P, 2, 2 * P], F32, tag="sums")
                for c in range(2):
                    rows_as_words = w_sb[j][:, 2 * half + c, :].bitcast(F32)
                    for u in range(2):
                        nc.tensor.transpose(bank[:, u, c * P : (c + 1) * P], rows_as_words[:, u * P : (u + 1) * P], ident[:])
                made["w_bank", j, half] = bank

        def copy_weight(j):
            w_grouped = work.tile([P, E * PACK], BF16, align_bytes=64)
            w_words = w_grouped[:].bitcast(F32).rearrange("i (p c u) -> i p c u", c=4, u=2)
            for half in range(2):
                nc.scalar.copy(
                    out=w_words[:, :, 2 * half : 2 * half + 2, :],
                    in_=made["w_bank", j, half][:].rearrange("i u (c p) -> i p c u", p=P),
                )
            made["w_grouped", j] = w_grouped

        def quantise_weight(j):
            nc.vector.quantize_mx(out=w_codes[:, j, :].bitcast(FP8X4), scales=w_scales[:, j, :], in_=made["w_grouped", j][:])

        def spread_bias(j):
            bias_bank = sums.tile([P, E], BF16, tag="sums")
            nc.tensor.matmul(out=bias_bank[:], lhsT=pick[:, j : j + 1].to_broadcast([P, P]), rhs=bias_rows[:], start=True, stop=True)
            made["bias_bank", j] = bias_bank

        def copy_bias(j):
            nc.scalar.copy(out=bias_all[:, j, :], in_=made["bias_bank", j][:])

        def statistics(n):
            stats = small.tile([P, GROUP, 6], F32)
            for i in range(GROUP):
                nc.vector.bn_stats(out=stats[:, i, :], in_=x_sb[stream_of(n)][:, tiles_of(n), :][:, i, :])
            made["stats", n] = stats

        def aggregate(n):
            mean_var = small.tile([P, GROUP, 2], F32)
            for i in range(GROUP):
                nc.vector.bn_aggr(out=mean_var[:, i, :], in_=made["stats", n][:, i, :])
            made["mean_var", n] = mean_var

        def sums_on_scalar(n):
            minus_mean = small.tile([P, GROUP], F32)
            x = x_sb[stream_of(n)][:, tiles_of(n), :]
            total = small.tile([P, GROUP], F32)
            squares = small.tile([P, GROUP], F32)
            junk = work.tile([P, D], BF16)
            for i in range(GROUP):
                nc.scalar.activation(out=junk[:], in_=x[:, i, :], func=ACT.Copy, accum_out=total[:, i : i + 1])
            nc.scalar.mul(out=minus_mean[:], in_=total[:], mul=-1.0 / D)
            for i in range(GROUP):
                nc.scalar.activation(out=junk[:], in_=x[:, i, :], func=ACT.Square, bias=minus_mean[:, i : i + 1], accum_out=squares[:, i : i + 1])
            rstd = small.tile([P, GROUP], F32)
            nc.scalar.activation(out=rstd[:], in_=squares[:], func=ACT.Abs_reciprocal_sqrt, bias=eps[:], scale=1.0 / D)
            made["rstd", n] = rstd
            made["offset", n] = minus_mean

        def rstd_and_mean(n):
            mean_var = made["mean_var", n]
            rstd = small.tile([P, GROUP], F32)
            nc.scalar.activation(out=rstd[:], in_=mean_var[:, :, 1], func=ACT.Abs_reciprocal_sqrt, bias=eps[:], scale=1.0)
            minus_mean = small.tile([P, GROUP], F32)
            nc.scalar.mul(out=minus_mean[:], in_=mean_var[:, :, 0], mul=-1.0)
            made["rstd", n] = rstd
            made["offset", n] = minus_mean

        def normalise(n):
            rstd = made["rstd", n]
            x_hat = work.tile([P, GROUP, D], F32)
            x = x_sb[stream_of(n)][:, tiles_of(n), :]
            offset = made["offset", n]
            for i in range(GROUP):
                nc.gpsimd.tensor_scalar(
                    out=x_hat[:, i, :].rearrange("p (u e q) -> p u e q", u=2, e=2),
                    in0=x[:, i, :].rearrange("p (u q e) -> p u e q", u=2, e=2),
                    scalar1=offset[:, i : i + 1],
                    scalar2=rstd[:, i : i + 1],
                    op0=ALU.add,
                    op1=ALU.mult,
                )
            made["x_hat", n] = x_hat

        def transpose_tokens(n):
            banks = [flip.tile([P, 2, TOKENS], F32, name="x_hat_t%d" % u, tag="flip") for u in range(2)]
            for i in range(GROUP):
                for t in range(PACK):
                    nc.tensor.transpose(
                        banks[t // 2][:, t % 2, i * P : (i + 1) * P], made["x_hat", n][:, i, t * P : (t + 1) * P], ident[:]
                    )
            made["banks", n] = banks

        def gain_and_shift(n):
            planes = work.tile([P, PACK, TOKENS], BF16)
            first = 2 * PACK * stream_of(n)
            for t in range(PACK):
                nc.scalar.activation(
                    out=planes[:, t, :],
                    in_=made["banks", n][t // 2][:, t % 2, :],
                    func=ACT.Identity,
                    scale=ln_cols[:, first + t : first + t + 1],
                    bias=ln_cols[:, first + PACK + t : first + PACK + t + 1],
                )
            made["planes", n] = planes

        def regroup(n):
            grouped = work.tile([P, TOKENS, PACK], BF16, align_bytes=64)
            nc.scalar.copy(
                out=grouped[:].rearrange("p (c m) t -> p c t m", m=4),
                in_=made["planes", n][:].rearrange("p t (c m) -> p c t m", m=4),
            )
            made["grouped", n] = grouped

        def quantise(n):
            codes = work.tile([P, TOKENS], U32, align_bytes=64)
            scales = work.tile([P, TOKENS], U8, align_bytes=64)
            nc.vector.quantize_mx(
                out=codes[:].bitcast(FP8X4), scales=scales[:], in_=made["grouped", n][:].rearrange("p c t -> p (c t)")
            )
            made["codes", n] = codes
            made["scales", n] = scales

        def multiply(n, o):
            for i in range(GROUP):
                j = qkv_of_stream[stream_of(n)][o]
                tokens = slice(i * P, (i + 1) * P)
                bank = sums.tile([P, E], F32, tag="sums")
                nc.tensor.matmul_mx(
                    out=bank[:],
                    lhsT=made["codes", n][:, tokens].bitcast(FP8X4),
                    lhsT_scale=made["scales", n][:, tokens],
                    rhs=w_codes[:, j, :].bitcast(FP8X4),
                    rhs_scale=w_scales[:, j, :],
                    start=True,
                    stop=True,
                )
                made["bank", n, o, i] = bank

        def add_bias(n, o):
            result = results.tile([P, GROUP, E], F32)
            for i in range(GROUP):
                j = qkv_of_stream[stream_of(n)][o]
                nc.vector.tensor_tensor(out=result[:, i, :], in0=made["bank", n, o, i][:], in1=bias_all[:, j, :], op=ALU.add)
            made["result", n, o] = result

        def store(n, o):
            nc.sync.dma_start(out=out_dram[o][stream_of(n), :, tiles_of(n), :], in_=made["result", n, o][:])

        def store_by_tile(n, o):
            for i in range(GROUP):
                tile = tiles_of(n).start + i
                nc.sync.dma_start(out=out_dram[o][stream_of(n), :, tile, :], in_=made["result", n, o][:, i, :])

        transpose_layer_norm_vectors()
        copy_layer_norm_vectors()
        statistics(0)
        aggregate(0)
        rstd_and_mean(0)
        normalise(0)
        transpose_weight(0)
        copy_weight(0)
        quantise_weight(0)
        spread_bias(0)
        copy_bias(0)
        statistics(1)
        aggregate(1)
        rstd_and_mean(1)
        normalise(1)
        transpose_tokens(0)
        gain_and_shift(0)
        regroup(0)
        quantise(0)
        transpose_weight(1)
        copy_weight(1)
        quantise_weight(1)
        spread_bias(1)
        copy_bias(1)
        statistics(2)
        aggregate(2)
        rstd_and_mean(2)
        normalise(2)
        transpose_tokens(1)
        gain_and_shift(1)
        regroup(1)
        quantise(1)
        multiply(0, 0)
        add_bias(0, 0)
        store(0, 0)
        transpose_weight(2)
        copy_weight(2)
        quantise_weight(2)
        spread_bias(2)
        copy_bias(2)
        statistics(3)
        aggregate(3)
        rstd_and_mean(3)
        normalise(3)
        multiply(0, 1)
        add_bias(0, 1)
        store(0, 1)
        multiply(1, 0)
        add_bias(1, 0)
        store(1, 0)
        multiply(1, 1)
        add_bias(1, 1)
        store(1, 1)
        transpose_tokens(2)
        gain_and_shift(2)
        regroup(2)
        quantise(2)
        transpose_weight(3)
        copy_weight(3)
        quantise_weight(3)
        spread_bias(3)
        copy_bias(3)
        statistics(4)
        aggregate(4)
        rstd_and_mean(4)
        normalise(4)
        multiply(0, 2)
        add_bias(0, 2)
        store(0, 2)
        multiply(1, 2)
        add_bias(1, 2)
        store(1, 2)
        transpose_tokens(3)
        gain_and_shift(3)
        regroup(3)
        quantise(3)
        transpose_weight(4)
        copy_weight(4)
        quantise_weight(4)
        spread_bias(4)
        copy_bias(4)
        statistics(5)
        aggregate(5)
        rstd_and_mean(5)
        normalise(5)
        multiply(2, 0)
        add_bias(2, 0)
        store(2, 0)
        multiply(2, 1)
        add_bias(2, 1)
        store(2, 1)
        multiply(2, 2)
        add_bias(2, 2)
        store(2, 2)
        sums_on_scalar(6)
        normalise(6)
        transpose_tokens(4)
        gain_and_shift(4)
        regroup(4)
        quantise(4)
        multiply(3, 0)
        add_bias(3, 0)
        store(3, 0)
        multiply(3, 1)
        add_bias(3, 1)
        store(3, 1)
        multiply(3, 2)
        add_bias(3, 2)
        store(3, 2)
        sums_on_scalar(7)
        normalise(7)
        transpose_tokens(5)
        gain_and_shift(5)
        regroup(5)
        quantise(5)
        multiply(4, 0)
        add_bias(4, 0)
        store(4, 0)
        multiply(4, 1)
        add_bias(4, 1)
        store(4, 1)
        multiply(4, 2)
        add_bias(4, 2)
        store(4, 2)
        transpose_tokens(6)
        gain_and_shift(6)
        regroup(6)
        quantise(6)
        multiply(5, 0)
        add_bias(5, 0)
        store(5, 0)
        multiply(5, 1)
        add_bias(5, 1)
        store(5, 1)
        multiply(5, 2)
        add_bias(5, 2)
        store(5, 2)
        transpose_tokens(7)
        gain_and_shift(7)
        regroup(7)
        quantise(7)
        multiply(6, 0)
        add_bias(6, 0)
        store(6, 0)
        multiply(6, 1)
        add_bias(6, 1)
        store(6, 1)
        multiply(6, 2)
        add_bias(6, 2)
        store(6, 2)
        multiply(7, 0)
        add_bias(7, 0)
        store(7, 0)
        multiply(7, 1)
        add_bias(7, 1)
        store(7, 1)
        multiply(7, 2)
        add_bias(7, 2)
        store(7, 2)
